import numpy as np
import ml_dtypes


def mxq(x, axis, fmt="e4m3"):
    dtype, down = {"e4m3": (ml_dtypes.float8_e4m3fn, 7), "e5m2": (ml_dtypes.float8_e5m2, 14)}[fmt]
    v = np.moveaxis(np.asarray(x, np.float32).astype(ml_dtypes.bfloat16).astype(np.float64), axis, -1)
    blocks = v.reshape(v.shape[:-1] + (-1, 32))
    amax = np.abs(blocks).max(-1, keepdims=True)
    byte = np.maximum(np.where(amax > 0, np.frexp(amax)[1] - 1 + 127, 0) - down, 1)
    scale = np.exp2(byte - 127.0)
    codes = (blocks / scale).astype(np.float32).astype(dtype).astype(np.float64)
    return np.moveaxis((codes * scale).reshape(v.shape), -1, axis)


WIDE = False


def mx_kscale(k):
    if not WIDE:
        return np.ones(k)
    levels = np.array([10, -10, 5, -5, 0])
    a = np.random.permutation(np.resize(levels, k // 512 * 4)).reshape(k // 512, 4)
    idx = np.arange(k)
    return np.exp2(a[idx // 512, idx % 128 // 32])


BF16 = ml_dtypes.bfloat16


def bf(x):
    return np.asarray(x, np.float32).astype(BF16)


def f64(x):
    return np.asarray(x).astype(np.float64)


B = 512
INPUTDIM = 256
OUTDIM = 256
GRIDSIZE = 64
KDIM = INPUTDIM * GRIDSIZE


def setup_inputs():
    scale = 1.0 / (np.sqrt(INPUTDIM) * np.sqrt(GRIDSIZE))
    t = mx_kscale(KDIM).reshape(INPUTDIM, GRIDSIZE)[:, 0]
    u = np.minimum(t, 1.0) ** 2
    k = np.arange(1, GRIDSIZE + 1).astype(np.float64)
    d = np.where(u[:, None] < 1.0, u[:, None] * k[None, :], 1.0)
    x = np.random.standard_normal((B, INPUTDIM)) * u
    w = np.random.standard_normal((2, OUTDIM, INPUTDIM, GRIDSIZE)) * scale
    w[1] = w[1] / d
    return {"x": bf(x),
            "fouriercoeffs": bf(w),
            "bias": bf(np.random.standard_normal((1, OUTDIM)) * 0.5)}


def reference(x, fouriercoeffs, bias):
    x = f64(x)
    w = f64(fouriercoeffs)
    k = np.arange(1, GRIDSIZE + 1).astype(np.float64)
    xk = x[:, :, None] * k
    c = np.cos(xk).reshape(x.shape[0], KDIM)
    s = np.sin(xk).reshape(x.shape[0], KDIM)
    w0 = w[0].reshape(OUTDIM, KDIM)
    w1 = w[1].reshape(OUTDIM, KDIM)
    y = mxq(c, 1, "e4m3") @ mxq(w0, 1, "e4m3").T
    y = y + (mxq(s, 1, "e4m3") @ mxq(w1, 1, "e4m3").T)
    y = y + f64(bias)
    return y

@@ -1,0 +1,167 @@
+import math
+
+import concourse.mybir as mybir
+from concourse.masks import make_identity
+
+F32 = mybir.dt.float32
+BF16 = mybir.dt.bfloat16
+I32 = mybir.dt.int32
+U32 = mybir.dt.uint32
+U8 = mybir.dt.uint8
+FP8X4 = mybir.dt.float8_e4m3fn_x4
+ALU = mybir.AluOpType
+ACT = mybir.ActivationFunctionType
+
+P = 128
+B = 512
+I_DIM = 256
+O_DIM = 256
+G_DIM = 64
+K_DIM = I_DIM * G_DIM
+PACK = 4
+K_PASS = P * PACK
+N_PASS = K_DIM // K_PASS
+GRP = 2
+N_GRP = N_PASS // GRP
+COLS = GRP * B
+BT = B // P
+
+FLOPS = 2 * B * O_DIM * 2 * K_DIM
+
+TWO_PI = 2.0 * math.pi
+INV_2PI = 1.0 / TWO_PI
+
+
+def tile_naivefourierkanlayer_kernel(tc, x, fouriercoeffs, bias, out):
+    nc = tc.nc
+    w_view = fouriercoeffs.rearrange("s (ot o) i g -> o (s ot) (i g)", o=P)
+
+    with tc.tile_pool(name="const", bufs=1) as const, \
+            tc.tile_pool(name="wload", bufs=2) as wload, \
+            tc.tile_pool(name="work", bufs=2) as work, \
+            tc.tile_pool(name="single", bufs=1) as single, \
+            tc.psum_pool(name="ypsum", bufs=1) as ypsum, \
+            tc.psum_pool(name="xpsum", bufs=2) as xpsum, \
+            tc.psum_pool(name="wpsum", bufs=2) as wpsum:
+
+        ident_b = const.tile([P, P], BF16)
+        make_identity(nc, ident_b[:])
+        ident_f = const.tile([P, P], F32)
+        make_identity(nc, ident_f[:])
+        sel = const.tile([P, P * 16], BF16)
+        nc.vector.tensor_copy(
+            out=sel[:].rearrange("p (j r) -> p j r", r=16),
+            in_=ident_b[:].unsqueeze(2).to_broadcast([P, P, 16]),
+        )
+        kidx = const.tile([P, PACK], I32)
+        nc.gpsimd.iota(kidx[:], pattern=[[1, PACK]], base=0, channel_multiplier=PACK)
+        kmod = const.tile([P, PACK], I32)
+        nc.vector.tensor_single_scalar(out=kmod[:], in_=kidx[:], scalar=G_DIM - 1, op=ALU.bitwise_and)
+        kf = const.tile([P, PACK], F32)
+        nc.vector.tensor_scalar(out=kf[:], in0=kmod[:], scalar1=1.0, scalar2=None, op0=ALU.add)
+        quarter = const.tile([P, 1], F32)
+        nc.vector.memset(quarter[:], 0.25)
+        halfpi = const.tile([P, 1], F32)
+        nc.vector.tensor_scalar(out=halfpi[:], in0=quarter[:], scalar1=TWO_PI, scalar2=None, op0=ALU.mult)
+
+        bias_b = const.tile([P, O_DIM], BF16)
+        nc.scalar.dma_start(out=bias_b[:], in_=bias.rearrange("o n -> (o n)").partition_broadcast(P))
+
+        xsb = const.tile([P, BT, I_DIM], BF16)
+        nc.sync.dma_start(out=xsb[:], in_=x.rearrange("(bt p) i -> p bt i", p=P))
+        xT = const.tile([P, 2, B], BF16)
+        for ih in range(2):
+            xt_ps = xpsum.tile([P, B], BF16, tag="xb")
+            for bt in range(BT):
+                nc.tensor.transpose(
+                    xt_ps[:, bt * P:(bt + 1) * P], xsb[:, bt, ih * P:(ih + 1) * P], ident_b[:]
+                )
+            nc.vector.tensor_copy(out=xT[:, ih, :], in_=xt_ps[:])
+
+        y_ps = [ypsum.tile([P, O_DIM], F32, name="y%d" % bt) for bt in range(BT)]
+
+        for g in range(N_GRP):
+            wraw = wload.tile([P, 4, GRP * K_PASS], BF16)
+            nc.sync.dma_start(out=wraw[:], in_=w_view[:, :, g * GRP * K_PASS:(g + 1) * GRP * K_PASS])
+            wwords = wraw[:].bitcast(F32)
+            wg = work.tile([P, 2 * GRP * O_DIM * PACK], BF16, align_bytes=64)
+            wg_words = wg[:].bitcast(F32)
+            for s in range(2):
+                for cc in range(GRP):
+                    wt_ps = wpsum.tile([P, 4, P], F32, tag="wt")
+                    for ot in range(2):
+                        for e in range(2):
+                            nc.tensor.transpose(
+                                wt_ps[:, ot * 2 + e, :],
+                                wwords[:, s * 2 + ot, cc * 256 + e:(cc + 1) * 256:2],
+                                ident_f[:],
+                            )
+                    blk = (s * GRP + cc) * 512
+                    nc.scalar.copy(
+                        out=wg_words[:, blk:blk + 512].rearrange("p (ot o e) -> p ot o e", ot=2, e=2),
+                        in_=wt_ps[:].rearrange("p (ot e) o -> p ot o e", e=2),
+                    )
+            wcodes = work.tile([P, 2 * GRP * O_DIM], U32, align_bytes=64)
+            wscales = work.tile([P, 2 * GRP * O_DIM], U8, align_bytes=64)
+            nc.vector.quantize_mx(out=wcodes[:].bitcast(FP8X4), scales=wscales[:], in_=wg[:])
+
+            theta = work.tile([P, PACK, COLS], F32)
+            for cc in range(GRP):
+                c = g * GRP + cc
+                xb_ps = xpsum.tile([P, B], F32, tag="xb")
+                nc.tensor.matmul(
+                    xb_ps[:], lhsT=sel[:, (c % 16) * P:(c % 16 + 1) * P], rhs=xT[:, c // 16, :],
+                    start=True, stop=True,
+                )
+                for t in range(PACK):
+                    nc.scalar.activation(
+                        out=theta[:, t, cc * B:(cc + 1) * B], in_=xb_ps[:], func=ACT.Copy, scale=kf[:, t:t + 1]
+                    )
+
+            nint = single.tile([P, PACK, COLS], I32)
+            nc.vector.tensor_scalar(out=nint[:], in0=theta[:], scalar1=INV_2PI, scalar2=None, op0=ALU.mult)
+            arg = work.tile([P, COLS * PACK], F32)
+            nc.vector.scalar_tensor_tensor(
+                out=arg[:].rearrange("p (n t) -> p n t", t=PACK),
+                in0=nint[:].rearrange("p t n -> p n t"), scalar=-TWO_PI,
+                in1=theta[:].rearrange("p t n -> p n t"),
+                op0=ALU.mult, op1=ALU.add,
+            )
+            aabs = work.tile([P, COLS * PACK], F32)
+            nc.vector.scalar_tensor_tensor(
+                out=aabs[:], in0=arg[:], scalar=-1.0, in1=arg[:], op0=ALU.mult, op1=ALU.max
+            )
+
+            sin_b = work.tile([P, COLS * PACK], BF16, align_bytes=64)
+            nc.scalar.activation(out=sin_b[:], in_=arg[:], func=ACT.Sin)
+            cos_b = work.tile([P, COLS * PACK], BF16, align_bytes=64)
+            nc.scalar.activation(out=cos_b[:], in_=aabs[:], func=ACT.Sin, bias=halfpi[:, 0:1], scale=-1.0)
+
+            ccodes = work.tile([P, COLS], U32, align_bytes=64)
+            cscales = work.tile([P, COLS], U8, align_bytes=64)
+            nc.vector.quantize_mx(out=ccodes[:].bitcast(FP8X4), scales=cscales[:], in_=cos_b[:])
+            scodes = work.tile([P, COLS], U32, align_bytes=64)
+            sscales = work.tile([P, COLS], U8, align_bytes=64)
+            nc.vector.quantize_mx(out=scodes[:].bitcast(FP8X4), scales=sscales[:], in_=sin_b[:])
+
+            for cc in range(GRP):
+                for s, (codes, scales) in enumerate(((ccodes, cscales), (scodes, sscales))):
+                    wcol = (s * GRP + cc) * O_DIM
+                    first = g == 0 and cc == 0 and s == 0
+                    last = g == N_GRP - 1 and cc == GRP - 1 and s == 1
+                    for bt in range(BT):
+                        col = cc * B + bt * P
+                        nc.tensor.matmul_mx(
+                            out=y_ps[bt][:],
+                            lhsT=codes[:, col:col + P].bitcast(FP8X4),
+                            lhsT_scale=scales[:, col:col + P],
+                            rhs=wcodes[:, wcol:wcol + O_DIM].bitcast(FP8X4),
+                            rhs_scale=wscales[:, wcol:wcol + O_DIM],
+                            start=first,
+                            stop=last,
+                        )
+
+        for bt in range(BT):
+            y_sb = work.tile([P, O_DIM], F32)
+            nc.vector.tensor_tensor(out=y_sb[:], in0=y_ps[bt][:], in1=bias_b[:], op=ALU.add)
+            nc.sync.dma_start(out=out[bt * P:(bt + 1) * P, :], in_=y_sb[:])

@@ -25,6 +25,8 @@ GRP = 2
 N_GRP = N_PASS // GRP
 COLS = GRP * B
 BT = B // P
+RUN = 4
+ABS_SCALAR = 2304
 
 FLOPS = 2 * B * O_DIM * 2 * K_DIM
 
@@ -105,37 +107,54 @@ def tile_naivefourierkanlayer_kernel(tc, x, fouriercoeffs, bias, out):
             wscales = work.tile([P, 2 * GRP * O_DIM], U8, align_bytes=64)
             nc.vector.quantize_mx(out=wcodes[:].bitcast(FP8X4), scales=wscales[:], in_=wg[:])
 
-            theta = work.tile([P, PACK, COLS], F32)
+            xb_ps = xpsum.tile([P, COLS], BF16, tag="xb")
             for cc in range(GRP):
                 c = g * GRP + cc
-                xb_ps = xpsum.tile([P, B], F32, tag="xb")
                 nc.tensor.matmul(
-                    xb_ps[:], lhsT=sel[:, (c % 16) * P:(c % 16 + 1) * P], rhs=xT[:, c // 16, :],
-                    start=True, stop=True,
+                    xb_ps[:, cc * B:(cc + 1) * B], lhsT=sel[:, (c % 16) * P:(c % 16 + 1) * P],
+                    rhs=xT[:, c // 16, :], start=True, stop=True,
                 )
-                for t in range(PACK):
-                    nc.scalar.activation(
-                        out=theta[:, t, cc * B:(cc + 1) * B], in_=xb_ps[:], func=ACT.Copy, scale=kf[:, t:t + 1]
-                    )
+            xs = work.tile([P, COLS], BF16)
+            nc.scalar.copy(out=xs[:], in_=xb_ps[:])
 
-            nint = single.tile([P, PACK, COLS], I32)
+            theta = work.tile([P, COLS * PACK], F32)
+            theta_qtf = theta[:].rearrange("p (q t f) -> p q t f", t=PACK, f=RUN)
+            for t in range(PACK):
+                nc.vector.tensor_scalar(
+                    out=theta_qtf[:, :, t, :], in0=xs[:].rearrange("p (q f) -> p q f", f=RUN),
+                    scalar1=kf[:, t:t + 1], scalar2=None, op0=ALU.mult,
+                )
+
+            nint = single.tile([P, COLS * PACK], I32)
             nc.vector.tensor_scalar(out=nint[:], in0=theta[:], scalar1=INV_2PI, scalar2=None, op0=ALU.mult)
             arg = work.tile([P, COLS * PACK], F32)
             nc.vector.scalar_tensor_tensor(
-                out=arg[:].rearrange("p (n t) -> p n t", t=PACK),
-                in0=nint[:].rearrange("p t n -> p n t"), scalar=-TWO_PI,
-                in1=theta[:].rearrange("p t n -> p n t"),
-                op0=ALU.mult, op1=ALU.add,
+                out=arg[:], in0=nint[:], scalar=-TWO_PI, in1=theta[:], op0=ALU.mult, op1=ALU.add
             )
-            aabs = work.tile([P, COLS * PACK], F32)
+            abs_s = work.tile([P, ABS_SCALAR], F32)
+            nc.scalar.activation(out=abs_s[:], in_=arg[:, 0:ABS_SCALAR], func=ACT.Abs)
+            abs_v = work.tile([P, COLS * PACK - ABS_SCALAR], F32)
             nc.vector.scalar_tensor_tensor(
-                out=aabs[:], in0=arg[:], scalar=-1.0, in1=arg[:], op0=ALU.mult, op1=ALU.max
+                out=abs_v[:], in0=arg[:, ABS_SCALAR:], scalar=-1.0, in1=arg[:, ABS_SCALAR:],
+                op0=ALU.mult, op1=ALU.max,
             )
 
             sin_b = work.tile([P, COLS * PACK], BF16, align_bytes=64)
-            nc.scalar.activation(out=sin_b[:], in_=arg[:], func=ACT.Sin)
+            nc.scalar.activation(
+                out=sin_b[:].rearrange("p (q f t) -> p q t f", f=RUN, t=PACK),
+                in_=arg[:].rearrange("p (q t f) -> p q t f", t=PACK, f=RUN), func=ACT.Sin,
+            )
             cos_b = work.tile([P, COLS * PACK], BF16, align_bytes=64)
-            nc.scalar.activation(out=cos_b[:], in_=aabs[:], func=ACT.Sin, bias=halfpi[:, 0:1], scale=-1.0)
+            nc.scalar.activation(
+                out=cos_b[:, 0:ABS_SCALAR].rearrange("p (q f t) -> p q t f", f=RUN, t=PACK),
+                in_=abs_s[:].rearrange("p (q t f) -> p q t f", t=PACK, f=RUN),
+                func=ACT.Sin, bias=halfpi[:, 0:1], scale=-1.0,
+            )
+            nc.scalar.activation(
+                out=cos_b[:, ABS_SCALAR:].rearrange("p (q f t) -> p q t f", f=RUN, t=PACK),
+                in_=abs_v[:].rearrange("p (q t f) -> p q t f", t=PACK, f=RUN),
+                func=ACT.Sin, bias=halfpi[:, 0:1], scale=-1.0,
+            )
 
             ccodes = work.tile([P, COLS], U32, align_bytes=64)
             cscales = work.tile([P, COLS], U8, align_bytes=64)

@@ -24,6 +24,7 @@ N_PASS = K_DIM // K_PASS
 GRP = 2
 N_GRP = N_PASS // GRP
 COLS = GRP * B
+WIDE = COLS * PACK
 BT = B // P
 RUN = 4
 ABS_SCALAR = 2304
@@ -39,24 +40,173 @@ def tile_naivefourierkanlayer_kernel(tc, x, fouriercoeffs, bias, out):
     w_view = fouriercoeffs.rearrange("s (ot o) i g -> o (s ot) (i g)", o=P)
 
     with tc.tile_pool(name="const", bufs=1) as const, \
-            tc.tile_pool(name="wload", bufs=2) as wload, \
-            tc.tile_pool(name="work", bufs=2) as work, \
-            tc.tile_pool(name="single", bufs=1) as single, \
+            tc.tile_pool(name="two", bufs=2) as two, \
+            tc.tile_pool(name="one", bufs=1) as one, \
             tc.psum_pool(name="ypsum", bufs=1) as ypsum, \
             tc.psum_pool(name="xpsum", bufs=2) as xpsum, \
-            tc.psum_pool(name="wpsum", bufs=2) as wpsum:
+            tc.psum_pool(name="wpsum", bufs=2) as wpsum, \
+            tc.manual_schedule():
+
+        live = {}
+
+        def load_w(g):
+            wraw = two.tile([P, 4, GRP * K_PASS], BF16, name="wraw")
+            nc.sync.dma_start(out=wraw[:], in_=w_view[:, :, g * GRP * K_PASS:(g + 1) * GRP * K_PASS])
+            live[("wraw", g)] = wraw
+
+        def spread_x(g):
+            xb_ps = xpsum.tile([P, COLS], BF16, name="xb")
+            for cc in range(GRP):
+                c = g * GRP + cc
+                nc.tensor.matmul(
+                    xb_ps[:, cc * B:(cc + 1) * B], lhsT=sel[:, (c % 16) * P:(c % 16 + 1) * P],
+                    rhs=xT[:, c // 16, :], start=True, stop=True,
+                )
+            live[("xb", g)] = xb_ps
+
+        def copy_x(g):
+            xs = two.tile([P, COLS], BF16, name="xs")
+            nc.scalar.copy(out=xs[:], in_=live[("xb", g)][:])
+            live[("xs", g)] = xs
+
+        def weights_piece(g, j):
+            if j == 0:
+                live[("wg", g)] = two.tile([P, 2 * GRP * O_DIM * PACK], BF16, name="wg", align_bytes=64)
+            s, cc = divmod(j, GRP)
+            wwords = live[("wraw", g)][:].bitcast(F32)
+            wt_ps = wpsum.tile([P, 4, P], F32, name="wt")
+            for ot in range(2):
+                for e in range(2):
+                    nc.tensor.transpose(
+                        wt_ps[:, ot * 2 + e, :],
+                        wwords[:, s * 2 + ot, cc * 256 + e:(cc + 1) * 256:2],
+                        ident_f[:],
+                    )
+            nc.scalar.copy(
+                out=live[("wg", g)][:].bitcast(F32)[:, j * 512:(j + 1) * 512].rearrange(
+                    "p (ot o e) -> p ot o e", ot=2, e=2),
+                in_=wt_ps[:].rearrange("p (ot e) o -> p ot o e", e=2),
+            )
+
+        def quantise_w(g):
+            wcodes = two.tile([P, 2 * GRP * O_DIM], U32, name="wcodes", align_bytes=64)
+            wscales = two.tile([P, 2 * GRP * O_DIM], U8, name="wscales", align_bytes=64)
+            nc.vector.quantize_mx(out=wcodes[:].bitcast(FP8X4), scales=wscales[:], in_=live[("wg", g)][:])
+            live[("w", g)] = (wcodes, wscales)
+
+        def angles(g):
+            xs = live[("xs", g)]
+            theta = one.tile([P, WIDE], F32, name="theta")
+            theta_qtf = theta[:].rearrange("p (q t f) -> p q t f", t=PACK, f=RUN)
+            for t in range(PACK):
+                nc.vector.tensor_scalar(
+                    out=theta_qtf[:, :, t, :], in0=xs[:].rearrange("p (q f) -> p q f", f=RUN),
+                    scalar1=kf[:, t:t + 1], scalar2=None, op0=ALU.mult,
+                )
+            live[("theta", g)] = theta
+
+        def turns(g):
+            nint = one.tile([P, WIDE], I32, name="nint")
+            nc.vector.tensor_scalar(
+                out=nint[:], in0=live[("theta", g)][:], scalar1=INV_2PI, scalar2=None, op0=ALU.mult
+            )
+            live[("nint", g)] = nint
+
+        def reduce_angles(g):
+            arg = two.tile([P, WIDE], F32, name="arg")
+            nc.vector.scalar_tensor_tensor(
+                out=arg[:], in0=live[("nint", g)][:], scalar=-TWO_PI, in1=live[("theta", g)][:],
+                op0=ALU.mult, op1=ALU.add,
+            )
+            live[("arg", g)] = arg
+
+        def abs_vector(g):
+            arg = live[("arg", g)]
+            abs_v = two.tile([P, WIDE - ABS_SCALAR], F32, name="abs_v")
+            nc.vector.scalar_tensor_tensor(
+                out=abs_v[:], in0=arg[:, ABS_SCALAR:], scalar=-1.0, in1=arg[:, ABS_SCALAR:],
+                op0=ALU.mult, op1=ALU.max,
+            )
+            live[("abs_v", g)] = abs_v
+
+        def qtf(ap):
+            return ap.rearrange("p (q t f) -> p q t f", t=PACK, f=RUN)
+
+        def qft(ap):
+            return ap.rearrange("p (q f t) -> p q t f", f=RUN, t=PACK)
+
+        def abs_scalar(g):
+            abs_s = one.tile([P, ABS_SCALAR], F32, name="abs_s")
+            nc.scalar.activation(out=abs_s[:], in_=live[("arg", g)][:, 0:ABS_SCALAR], func=ACT.Abs)
+            live[("abs_s", g)] = abs_s
+
+        def sine(g):
+            sin_b = two.tile([P, WIDE], BF16, name="sin_b", align_bytes=64)
+            nc.scalar.activation(out=qft(sin_b[:]), in_=qtf(live[("arg", g)][:]), func=ACT.Sin)
+            live[("sin", g)] = sin_b
+
+        def cosine_s(g):
+            cos_b = two.tile([P, WIDE], BF16, name="cos_b", align_bytes=64)
+            nc.scalar.activation(
+                out=qft(cos_b[:, 0:ABS_SCALAR]), in_=qtf(live[("abs_s", g)][:]),
+                func=ACT.Sin, bias=halfpi[:, 0:1], scale=-1.0,
+            )
+            live[("cos", g)] = cos_b
+
+        def cosine_v(g):
+            nc.scalar.activation(
+                out=qft(live[("cos", g)][:, ABS_SCALAR:]), in_=qtf(live[("abs_v", g)][:]),
+                func=ACT.Sin, bias=halfpi[:, 0:1], scale=-1.0,
+            )
+
+        def quantise_basis(g, which):
+            codes = two.tile([P, COLS], U32, name=which + "_codes", align_bytes=64)
+            scales = two.tile([P, COLS], U8, name=which + "_scales", align_bytes=64)
+            nc.vector.quantize_mx(out=codes[:].bitcast(FP8X4), scales=scales[:], in_=live[(which, g)][:])
+            live[(which + "q", g)] = (codes, scales)
+
+        def multiply(g):
+            wcodes, wscales = live[("w", g)]
+            for s, which in enumerate(("cosq", "sinq")):
+                codes, scales = live[(which, g)]
+                order = 1 - s
+                for cc in range(GRP):
+                    wcol = (s * GRP + cc) * O_DIM
+                    for bt in range(BT):
+                        col = cc * B + bt * P
+                        live[("mx", order, cc, bt)] = (codes, scales, col, wcol)
+            for order in range(2):
+                for cc in range(GRP):
+                    for bt in range(BT):
+                        codes, scales, col, wcol = live[("mx", order, cc, bt)]
+                        nc.tensor.matmul_mx(
+                            out=y_ps[bt][:],
+                            lhsT=codes[:, col:col + P].bitcast(FP8X4),
+                            lhsT_scale=scales[:, col:col + P],
+                            rhs=wcodes[:, wcol:wcol + O_DIM].bitcast(FP8X4),
+                            rhs_scale=wscales[:, wcol:wcol + O_DIM],
+                            start=(g == 0 and order == 0 and cc == 0),
+                            stop=(g == N_GRP - 1 and order == 1 and cc == GRP - 1),
+                        )
+
+        xsb = const.tile([P, BT, I_DIM], BF16)
+        nc.sync.dma_start(out=xsb[:], in_=x.rearrange("(bt p) i -> p bt i", p=P))
+        load_w(0)
+        load_w(1)
+        bias_b = const.tile([P, O_DIM], BF16)
+        nc.sync.dma_start(out=bias_b[:], in_=bias.rearrange("o n -> (o n)").partition_broadcast(P))
 
         ident_b = const.tile([P, P], BF16)
         make_identity(nc, ident_b[:])
         ident_f = const.tile([P, P], F32)
         make_identity(nc, ident_f[:])
+        kidx = const.tile([P, PACK], I32)
+        nc.gpsimd.iota(kidx[:], pattern=[[1, PACK]], base=0, channel_multiplier=PACK)
         sel = const.tile([P, P * 16], BF16)
         nc.vector.tensor_copy(
             out=sel[:].rearrange("p (j r) -> p j r", r=16),
             in_=ident_b[:].unsqueeze(2).to_broadcast([P, P, 16]),
         )
-        kidx = const.tile([P, PACK], I32)
-        nc.gpsimd.iota(kidx[:], pattern=[[1, PACK]], base=0, channel_multiplier=PACK)
         kmod = const.tile([P, PACK], I32)
         nc.vector.tensor_single_scalar(out=kmod[:], in_=kidx[:], scalar=G_DIM - 1, op=ALU.bitwise_and)
         kf = const.tile([P, PACK], F32)
@@ -66,14 +216,9 @@ def tile_naivefourierkanlayer_kernel(tc, x, fouriercoeffs, bias, out):
         halfpi = const.tile([P, 1], F32)
         nc.vector.tensor_scalar(out=halfpi[:], in0=quarter[:], scalar1=TWO_PI, scalar2=None, op0=ALU.mult)
 
-        bias_b = const.tile([P, O_DIM], BF16)
-        nc.scalar.dma_start(out=bias_b[:], in_=bias.rearrange("o n -> (o n)").partition_broadcast(P))
-
-        xsb = const.tile([P, BT, I_DIM], BF16)
-        nc.sync.dma_start(out=xsb[:], in_=x.rearrange("(bt p) i -> p bt i", p=P))
         xT = const.tile([P, 2, B], BF16)
         for ih in range(2):
-            xt_ps = xpsum.tile([P, B], BF16, tag="xb")
+            xt_ps = xpsum.tile([P, B], BF16, name="xb")
             for bt in range(BT):
                 nc.tensor.transpose(
                     xt_ps[:, bt * P:(bt + 1) * P], xsb[:, bt, ih * P:(ih + 1) * P], ident_b[:]
@@ -82,105 +227,48 @@ def tile_naivefourierkanlayer_kernel(tc, x, fouriercoeffs, bias, out):
 
         y_ps = [ypsum.tile([P, O_DIM], F32, name="y%d" % bt) for bt in range(BT)]
 
-        for g in range(N_GRP):
-            wraw = wload.tile([P, 4, GRP * K_PASS], BF16)
-            nc.sync.dma_start(out=wraw[:], in_=w_view[:, :, g * GRP * K_PASS:(g + 1) * GRP * K_PASS])
-            wwords = wraw[:].bitcast(F32)
-            wg = work.tile([P, 2 * GRP * O_DIM * PACK], BF16, align_bytes=64)
-            wg_words = wg[:].bitcast(F32)
-            for s in range(2):
-                for cc in range(GRP):
-                    wt_ps = wpsum.tile([P, 4, P], F32, tag="wt")
-                    for ot in range(2):
-                        for e in range(2):
-                            nc.tensor.transpose(
-                                wt_ps[:, ot * 2 + e, :],
-                                wwords[:, s * 2 + ot, cc * 256 + e:(cc + 1) * 256:2],
-                                ident_f[:],
-                            )
-                    blk = (s * GRP + cc) * 512
-                    nc.scalar.copy(
-                        out=wg_words[:, blk:blk + 512].rearrange("p (ot o e) -> p ot o e", ot=2, e=2),
-                        in_=wt_ps[:].rearrange("p (ot e) o -> p ot o e", e=2),
-                    )
-            wcodes = work.tile([P, 2 * GRP * O_DIM], U32, align_bytes=64)
-            wscales = work.tile([P, 2 * GRP * O_DIM], U8, align_bytes=64)
-            nc.vector.quantize_mx(out=wcodes[:].bitcast(FP8X4), scales=wscales[:], in_=wg[:])
-
-            xb_ps = xpsum.tile([P, COLS], BF16, tag="xb")
-            for cc in range(GRP):
-                c = g * GRP + cc
-                nc.tensor.matmul(
-                    xb_ps[:, cc * B:(cc + 1) * B], lhsT=sel[:, (c % 16) * P:(c % 16 + 1) * P],
-                    rhs=xT[:, c // 16, :], start=True, stop=True,
-                )
-            xs = work.tile([P, COLS], BF16)
-            nc.scalar.copy(out=xs[:], in_=xb_ps[:])
-
-            theta = work.tile([P, COLS * PACK], F32)
-            theta_qtf = theta[:].rearrange("p (q t f) -> p q t f", t=PACK, f=RUN)
-            for t in range(PACK):
-                nc.vector.tensor_scalar(
-                    out=theta_qtf[:, :, t, :], in0=xs[:].rearrange("p (q f) -> p q f", f=RUN),
-                    scalar1=kf[:, t:t + 1], scalar2=None, op0=ALU.mult,
-                )
-
-            nint = single.tile([P, COLS * PACK], I32)
-            nc.vector.tensor_scalar(out=nint[:], in0=theta[:], scalar1=INV_2PI, scalar2=None, op0=ALU.mult)
-            arg = work.tile([P, COLS * PACK], F32)
-            nc.vector.scalar_tensor_tensor(
-                out=arg[:], in0=nint[:], scalar=-TWO_PI, in1=theta[:], op0=ALU.mult, op1=ALU.add
-            )
-            abs_s = work.tile([P, ABS_SCALAR], F32)
-            nc.scalar.activation(out=abs_s[:], in_=arg[:, 0:ABS_SCALAR], func=ACT.Abs)
-            abs_v = work.tile([P, COLS * PACK - ABS_SCALAR], F32)
-            nc.vector.scalar_tensor_tensor(
-                out=abs_v[:], in0=arg[:, ABS_SCALAR:], scalar=-1.0, in1=arg[:, ABS_SCALAR:],
-                op0=ALU.mult, op1=ALU.max,
-            )
-
-            sin_b = work.tile([P, COLS * PACK], BF16, align_bytes=64)
-            nc.scalar.activation(
-                out=sin_b[:].rearrange("p (q f t) -> p q t f", f=RUN, t=PACK),
-                in_=arg[:].rearrange("p (q t f) -> p q t f", t=PACK, f=RUN), func=ACT.Sin,
-            )
-            cos_b = work.tile([P, COLS * PACK], BF16, align_bytes=64)
-            nc.scalar.activation(
-                out=cos_b[:, 0:ABS_SCALAR].rearrange("p (q f t) -> p q t f", f=RUN, t=PACK),
-                in_=abs_s[:].rearrange("p (q t f) -> p q t f", t=PACK, f=RUN),
-                func=ACT.Sin, bias=halfpi[:, 0:1], scale=-1.0,
-            )
-            nc.scalar.activation(
-                out=cos_b[:, ABS_SCALAR:].rearrange("p (q f t) -> p q t f", f=RUN, t=PACK),
-                in_=abs_v[:].rearrange("p (q t f) -> p q t f", t=PACK, f=RUN),
-                func=ACT.Sin, bias=halfpi[:, 0:1], scale=-1.0,
-            )
-
-            ccodes = work.tile([P, COLS], U32, align_bytes=64)
-            cscales = work.tile([P, COLS], U8, align_bytes=64)
-            nc.vector.quantize_mx(out=ccodes[:].bitcast(FP8X4), scales=cscales[:], in_=cos_b[:])
-            scodes = work.tile([P, COLS], U32, align_bytes=64)
-            sscales = work.tile([P, COLS], U8, align_bytes=64)
-            nc.vector.quantize_mx(out=scodes[:].bitcast(FP8X4), scales=sscales[:], in_=sin_b[:])
-
-            for cc in range(GRP):
-                for s, (codes, scales) in enumerate(((ccodes, cscales), (scodes, sscales))):
-                    wcol = (s * GRP + cc) * O_DIM
-                    first = g == 0 and cc == 0 and s == 0
-                    last = g == N_GRP - 1 and cc == GRP - 1 and s == 1
-                    for bt in range(BT):
-                        col = cc * B + bt * P
-                        nc.tensor.matmul_mx(
-                            out=y_ps[bt][:],
-                            lhsT=codes[:, col:col + P].bitcast(FP8X4),
-                            lhsT_scale=scales[:, col:col + P],
-                            rhs=wcodes[:, wcol:wcol + O_DIM].bitcast(FP8X4),
-                            rhs_scale=wscales[:, wcol:wcol + O_DIM],
-                            start=first,
-                            stop=last,
-                        )
+        for j in range(-2, N_GRP):
+            ahead = j + 2
+            if j >= 1:
+                multiply(j - 1)
+            if 2 <= ahead + 1 < N_GRP and j >= -1:
+                load_w(ahead + 1)
+            if ahead < N_GRP:
+                spread_x(ahead)
+                if j < 0:
+                    copy_x(ahead)
+            if j >= 0:
+                abs_scalar(j)
+                sine(j)
+            if ahead < N_GRP:
+                weights_piece(ahead, 0)
+            if j >= 0:
+                cosine_s(j)
+            if ahead < N_GRP:
+                weights_piece(ahead, 1)
+            if j >= 0:
+                cosine_v(j)
+            if ahead < N_GRP:
+                weights_piece(ahead, 2)
+                weights_piece(ahead, 3)
+                if j >= 0:
+                    copy_x(ahead)
+            nxt = 0 <= j + 1 < N_GRP
+            if nxt:
+                angles(j + 1)
+                quantise_w(j + 1)
+                turns(j + 1)
+            if j >= 0:
+                quantise_basis(j, "sin")
+            if nxt:
+                reduce_angles(j + 1)
+            if j >= 0:
+                quantise_basis(j, "cos")
+            if nxt:
+                abs_vector(j + 1)
+        multiply(N_GRP - 1)
 
         for bt in range(BT):
-            y_sb = work.tile([P, O_DIM], F32)
+            y_sb = two.tile([P, O_DIM], F32, name="y_sb")
             nc.vector.tensor_tensor(out=y_sb[:], in0=y_ps[bt][:], in1=bias_b[:], op=ALU.add)
             nc.sync.dma_start(out=out[bt * P:(bt + 1) * P, :], in_=y_sb[:])

@@ -22,12 +22,14 @@ PACK = 4
 K_PASS = P * PACK
 N_PASS = K_DIM // K_PASS
 GRP = 2
-N_GRP = N_PASS // GRP
+SIZES = [1] + [GRP] * ((N_PASS - 2) // GRP) + [1]
+N_GRP = len(SIZES)
+FIRST = [sum(SIZES[:g]) for g in range(N_GRP)]
 COLS = GRP * B
 WIDE = COLS * PACK
 BT = B // P
 RUN = 4
-ABS_SCALAR = 2304
+ABS_SCALAR = [B * PACK] + [2560] * (N_GRP - 3) + [1536, 512]
 
 FLOPS = 2 * B * O_DIM * 2 * K_DIM
 
@@ -49,15 +51,27 @@ def tile_naivefourierkanlayer_kernel(tc, x, fouriercoeffs, bias, out):
 
         live = {}
 
+        def wide(g):
+            return SIZES[g] * B * PACK
+
+        def qtf(ap):
+            return ap.rearrange("p (q t f) -> p q t f", t=PACK, f=RUN)
+
+        def qft(ap):
+            return ap.rearrange("p (q f t) -> p q t f", f=RUN, t=PACK)
+
         def load_w(g):
             wraw = two.tile([P, 4, GRP * K_PASS], BF16, name="wraw")
-            nc.sync.dma_start(out=wraw[:], in_=w_view[:, :, g * GRP * K_PASS:(g + 1) * GRP * K_PASS])
+            nc.sync.dma_start(
+                out=wraw[:, :, 0:SIZES[g] * K_PASS],
+                in_=w_view[:, :, FIRST[g] * K_PASS:(FIRST[g] + SIZES[g]) * K_PASS],
+            )
             live[("wraw", g)] = wraw
 
         def spread_x(g):
             xb_ps = xpsum.tile([P, COLS], BF16, name="xb")
-            for cc in range(GRP):
-                c = g * GRP + cc
+            for cc in range(SIZES[g]):
+                c = FIRST[g] + cc
                 nc.tensor.matmul(
                     xb_ps[:, cc * B:(cc + 1) * B], lhsT=sel[:, (c % 16) * P:(c % 16 + 1) * P],
                     rhs=xT[:, c // 16, :], start=True, stop=True,
@@ -66,13 +80,13 @@ def tile_naivefourierkanlayer_kernel(tc, x, fouriercoeffs, bias, out):
 
         def copy_x(g):
             xs = two.tile([P, COLS], BF16, name="xs")
-            nc.scalar.copy(out=xs[:], in_=live[("xb", g)][:])
+            nc.scalar.copy(out=xs[:, 0:SIZES[g] * B], in_=live[("xb", g)][:, 0:SIZES[g] * B])
             live[("xs", g)] = xs
 
         def weights_piece(g, j):
             if j == 0:
                 live[("wg", g)] = two.tile([P, 2 * GRP * O_DIM * PACK], BF16, name="wg", align_bytes=64)
-            s, cc = divmod(j, GRP)
+            s, cc = divmod(j, SIZES[g])
             wwords = live[("wraw", g)][:].bitcast(F32)
             wt_ps = wpsum.tile([P, 4, P], F32, name="wt")
             for ot in range(2):
@@ -91,16 +105,19 @@ def tile_naivefourierkanlayer_kernel(tc, x, fouriercoeffs, bias, out):
         def quantise_w(g):
             wcodes = two.tile([P, 2 * GRP * O_DIM], U32, name="wcodes", align_bytes=64)
             wscales = two.tile([P, 2 * GRP * O_DIM], U8, name="wscales", align_bytes=64)
-            nc.vector.quantize_mx(out=wcodes[:].bitcast(FP8X4), scales=wscales[:], in_=live[("wg", g)][:])
+            n = 2 * SIZES[g] * O_DIM
+            nc.vector.quantize_mx(
+                out=wcodes[:, 0:n].bitcast(FP8X4), scales=wscales[:, 0:n], in_=live[("wg", g)][:, 0:n * PACK]
+            )
             live[("w", g)] = (wcodes, wscales)
 
         def angles(g):
             xs = live[("xs", g)]
             theta = one.tile([P, WIDE], F32, name="theta")
-            theta_qtf = theta[:].rearrange("p (q t f) -> p q t f", t=PACK, f=RUN)
+            theta_qtf = qtf(theta[:, 0:wide(g)])
             for t in range(PACK):
                 nc.vector.tensor_scalar(
-                    out=theta_qtf[:, :, t, :], in0=xs[:].rearrange("p (q f) -> p q f", f=RUN),
+                    out=theta_qtf[:, :, t, :], in0=xs[:, 0:SIZES[g] * B].rearrange("p (q f) -> p q f", f=RUN),
                     scalar1=kf[:, t:t + 1], scalar2=None, op0=ALU.mult,
                 )
             live[("theta", g)] = theta
@@ -108,85 +125,79 @@ def tile_naivefourierkanlayer_kernel(tc, x, fouriercoeffs, bias, out):
         def turns(g):
             nint = one.tile([P, WIDE], I32, name="nint")
             nc.vector.tensor_scalar(
-                out=nint[:], in0=live[("theta", g)][:], scalar1=INV_2PI, scalar2=None, op0=ALU.mult
+                out=nint[:, 0:wide(g)], in0=live[("theta", g)][:, 0:wide(g)], scalar1=INV_2PI, scalar2=None,
+                op0=ALU.mult,
             )
             live[("nint", g)] = nint
 
         def reduce_angles(g):
             arg = two.tile([P, WIDE], F32, name="arg")
             nc.vector.scalar_tensor_tensor(
-                out=arg[:], in0=live[("nint", g)][:], scalar=-TWO_PI, in1=live[("theta", g)][:],
-                op0=ALU.mult, op1=ALU.add,
+                out=arg[:, 0:wide(g)], in0=live[("nint", g)][:, 0:wide(g)], scalar=-TWO_PI,
+                in1=live[("theta", g)][:, 0:wide(g)], op0=ALU.mult, op1=ALU.add,
             )
             live[("arg", g)] = arg
 
         def abs_vector(g):
-            arg = live[("arg", g)]
-            abs_v = two.tile([P, WIDE - ABS_SCALAR], F32, name="abs_v")
+            rest = live[("arg", g)][:, ABS_SCALAR[g]:wide(g)]
+            abs_v = two.tile([P, WIDE], F32, name="abs_v")
             nc.vector.scalar_tensor_tensor(
-                out=abs_v[:], in0=arg[:, ABS_SCALAR:], scalar=-1.0, in1=arg[:, ABS_SCALAR:],
-                op0=ALU.mult, op1=ALU.max,
+                out=abs_v[:, ABS_SCALAR[g]:wide(g)], in0=rest, scalar=-1.0, in1=rest, op0=ALU.mult, op1=ALU.max
             )
             live[("abs_v", g)] = abs_v
 
-        def qtf(ap):
-            return ap.rearrange("p (q t f) -> p q t f", t=PACK, f=RUN)
-
-        def qft(ap):
-            return ap.rearrange("p (q f t) -> p q t f", f=RUN, t=PACK)
-
         def abs_scalar(g):
-            abs_s = one.tile([P, ABS_SCALAR], F32, name="abs_s")
-            nc.scalar.activation(out=abs_s[:], in_=live[("arg", g)][:, 0:ABS_SCALAR], func=ACT.Abs)
+            abs_s = one.tile([P, WIDE], F32, name="abs_s")
+            nc.scalar.activation(
+                out=abs_s[:, 0:ABS_SCALAR[g]], in_=live[("arg", g)][:, 0:ABS_SCALAR[g]], func=ACT.Abs
+            )
             live[("abs_s", g)] = abs_s
 
         def sine(g):
             sin_b = two.tile([P, WIDE], BF16, name="sin_b", align_bytes=64)
-            nc.scalar.activation(out=qft(sin_b[:]), in_=qtf(live[("arg", g)][:]), func=ACT.Sin)
+            nc.scalar.activation(out=qft(sin_b[:, 0:wide(g)]), in_=qtf(live[("arg", g)][:, 0:wide(g)]), func=ACT.Sin)
             live[("sin", g)] = sin_b
 
         def cosine_s(g):
             cos_b = two.tile([P, WIDE], BF16, name="cos_b", align_bytes=64)
             nc.scalar.activation(
-                out=qft(cos_b[:, 0:ABS_SCALAR]), in_=qtf(live[("abs_s", g)][:]),
+                out=qft(cos_b[:, 0:ABS_SCALAR[g]]), in_=qtf(live[("abs_s", g)][:, 0:ABS_SCALAR[g]]),
                 func=ACT.Sin, bias=halfpi[:, 0:1], scale=-1.0,
             )
             live[("cos", g)] = cos_b
 
         def cosine_v(g):
             nc.scalar.activation(
-                out=qft(live[("cos", g)][:, ABS_SCALAR:]), in_=qtf(live[("abs_v", g)][:]),
+                out=qft(live[("cos", g)][:, ABS_SCALAR[g]:wide(g)]),
+                in_=qtf(live[("abs_v", g)][:, ABS_SCALAR[g]:wide(g)]),
                 func=ACT.Sin, bias=halfpi[:, 0:1], scale=-1.0,
             )
 
         def quantise_basis(g, which):
             codes = two.tile([P, COLS], U32, name=which + "_codes", align_bytes=64)
             scales = two.tile([P, COLS], U8, name=which + "_scales", align_bytes=64)
-            nc.vector.quantize_mx(out=codes[:].bitcast(FP8X4), scales=scales[:], in_=live[(which, g)][:])
+            n = SIZES[g] * B
+            nc.vector.quantize_mx(
+                out=codes[:, 0:n].bitcast(FP8X4), scales=scales[:, 0:n], in_=live[(which, g)][:, 0:n * PACK]
+            )
             live[(which + "q", g)] = (codes, scales)
 
         def multiply(g):
             wcodes, wscales = live[("w", g)]
-            for s, which in enumerate(("cosq", "sinq")):
+            for s, which in ((1, "sinq"), (0, "cosq")):
                 codes, scales = live[(which, g)]
-                order = 1 - s
-                for cc in range(GRP):
-                    wcol = (s * GRP + cc) * O_DIM
+                for cc in range(SIZES[g]):
+                    wcol = (s * SIZES[g] + cc) * O_DIM
                     for bt in range(BT):
                         col = cc * B + bt * P
-                        live[("mx", order, cc, bt)] = (codes, scales, col, wcol)
-            for order in range(2):
-                for cc in range(GRP):
-                    for bt in range(BT):
-                        codes, scales, col, wcol = live[("mx", order, cc, bt)]
                         nc.tensor.matmul_mx(
                             out=y_ps[bt][:],
                             lhsT=codes[:, col:col + P].bitcast(FP8X4),
                             lhsT_scale=scales[:, col:col + P],
                             rhs=wcodes[:, wcol:wcol + O_DIM].bitcast(FP8X4),
                             rhs_scale=wscales[:, wcol:wcol + O_DIM],
-                            start=(g == 0 and order == 0 and cc == 0),
-                            stop=(g == N_GRP - 1 and order == 1 and cc == GRP - 1),
+                            start=(g == 0 and s == 1 and cc == 0),
+                            stop=(g == N_GRP - 1 and s == 0 and cc == SIZES[g] - 1),
                         )
 
         xsb = const.tile([P, BT, I_DIM], BF16)
@@ -217,7 +228,8 @@ def tile_naivefourierkanlayer_kernel(tc, x, fouriercoeffs, bias, out):
         nc.vector.tensor_scalar(out=halfpi[:], in0=quarter[:], scalar1=TWO_PI, scalar2=None, op0=ALU.mult)
 
         xT = const.tile([P, 2, B], BF16)
-        for ih in range(2):
+
+        def transpose_x(ih):
             xt_ps = xpsum.tile([P, B], BF16, name="xb")
             for bt in range(BT):
                 nc.tensor.transpose(
@@ -225,34 +237,37 @@ def tile_naivefourierkanlayer_kernel(tc, x, fouriercoeffs, bias, out):
                 )
             nc.vector.tensor_copy(out=xT[:, ih, :], in_=xt_ps[:])
 
+        transpose_x(0)
+
         y_ps = [ypsum.tile([P, O_DIM], F32, name="y%d" % bt) for bt in range(BT)]
 
         for j in range(-2, N_GRP):
             ahead = j + 2
+            pieces = list(range(2 * SIZES[ahead])) if ahead < N_GRP else []
             if j >= 1:
                 multiply(j - 1)
-            if 2 <= ahead + 1 < N_GRP and j >= -1:
+            if j >= -1 and ahead + 1 < N_GRP:
                 load_w(ahead + 1)
             if ahead < N_GRP:
                 spread_x(ahead)
                 if j < 0:
                     copy_x(ahead)
             if j >= 0:
-                abs_scalar(j)
+                if ABS_SCALAR[j] > 0:
+                    abs_scalar(j)
                 sine(j)
-            if ahead < N_GRP:
-                weights_piece(ahead, 0)
+            for piece in pieces[0:1]:
+                weights_piece(ahead, piece)
             if j >= 0:
                 cosine_s(j)
-            if ahead < N_GRP:
-                weights_piece(ahead, 1)
-            if j >= 0:
+            for piece in pieces[1:2]:
+                weights_piece(ahead, piece)
+            if j >= 0 and ABS_SCALAR[j] < wide(j):
                 cosine_v(j)
-            if ahead < N_GRP:
-                weights_piece(ahead, 2)
-                weights_piece(ahead, 3)
-                if j >= 0:
-                    copy_x(ahead)
+            for piece in pieces[2:]:
+                weights_piece(ahead, piece)
+            if ahead < N_GRP and j >= 0:
+                copy_x(ahead)
             nxt = 0 <= j + 1 < N_GRP
             if nxt:
                 angles(j + 1)
@@ -264,8 +279,10 @@ def tile_naivefourierkanlayer_kernel(tc, x, fouriercoeffs, bias, out):
                 reduce_angles(j + 1)
             if j >= 0:
                 quantise_basis(j, "cos")
-            if nxt:
+            if nxt and ABS_SCALAR[j + 1] < wide(j + 1):
                 abs_vector(j + 1)
+            if j == 0:
+                transpose_x(1)
         multiply(N_GRP - 1)
 
         for bt in range(BT):

@@ -29,7 +29,10 @@ COLS = GRP * B
 WIDE = COLS * PACK
 BT = B // P
 RUN = 4
-ABS_SCALAR = [B * PACK] + [2560] * (N_GRP - 3) + [1536, 512]
+ABS_SCALAR = [B * PACK] + [2816] * (N_GRP - 3) + [1536, 512]
+ABS_S_MAX = max(ABS_SCALAR)
+ABS_V_MAX = max(SIZES[g] * B * PACK - ABS_SCALAR[g] for g in range(N_GRP))
+BY_MATMUL = 2
 
 FLOPS = 2 * B * O_DIM * 2 * K_DIM
 
@@ -44,6 +47,7 @@ def tile_naivefourierkanlayer_kernel(tc, x, fouriercoeffs, bias, out):
     with tc.tile_pool(name="const", bufs=1) as const, \
             tc.tile_pool(name="two", bufs=2) as two, \
             tc.tile_pool(name="one", bufs=1) as one, \
+            tc.tile_pool(name="three", bufs=3) as three, \
             tc.psum_pool(name="ypsum", bufs=1) as ypsum, \
             tc.psum_pool(name="xpsum", bufs=2) as xpsum, \
             tc.psum_pool(name="wpsum", bufs=2) as wpsum, \
@@ -81,6 +85,16 @@ def tile_naivefourierkanlayer_kernel(tc, x, fouriercoeffs, bias, out):
         def copy_x(g):
             xs = two.tile([P, COLS], BF16, name="xs")
             nc.scalar.copy(out=xs[:, 0:SIZES[g] * B], in_=live[("xb", g)][:, 0:SIZES[g] * B])
+            live[("xs", g)] = xs
+
+        def fetch_x(g):
+            xs = three.tile([P, COLS], F32, name="xs32")
+            for cc in range(SIZES[g]):
+                for il in range(8):
+                    nc.sync.dma_start(
+                        out=xs[il * 16:(il + 1) * 16, cc * B:(cc + 1) * B],
+                        in_=out_rows[(FIRST[g] + cc) * 8 + il, :].partition_broadcast(16),
+                    )
             live[("xs", g)] = xs
 
         def weights_piece(g, j):
@@ -140,14 +154,14 @@ def tile_naivefourierkanlayer_kernel(tc, x, fouriercoeffs, bias, out):
 
         def abs_vector(g):
             rest = live[("arg", g)][:, ABS_SCALAR[g]:wide(g)]
-            abs_v = two.tile([P, WIDE], F32, name="abs_v")
+            abs_v = two.tile([P, ABS_V_MAX], F32, name="abs_v")
             nc.vector.scalar_tensor_tensor(
-                out=abs_v[:, ABS_SCALAR[g]:wide(g)], in0=rest, scalar=-1.0, in1=rest, op0=ALU.mult, op1=ALU.max
+                out=abs_v[:, 0:wide(g) - ABS_SCALAR[g]], in0=rest, scalar=-1.0, in1=rest, op0=ALU.mult, op1=ALU.max
             )
             live[("abs_v", g)] = abs_v
 
         def abs_scalar(g):
-            abs_s = one.tile([P, WIDE], F32, name="abs_s")
+            abs_s = one.tile([P, ABS_S_MAX], F32, name="abs_s")
             nc.scalar.activation(
                 out=abs_s[:, 0:ABS_SCALAR[g]], in_=live[("arg", g)][:, 0:ABS_SCALAR[g]], func=ACT.Abs
             )
@@ -169,7 +183,7 @@ def tile_naivefourierkanlayer_kernel(tc, x, fouriercoeffs, bias, out):
         def cosine_v(g):
             nc.scalar.activation(
                 out=qft(live[("cos", g)][:, ABS_SCALAR[g]:wide(g)]),
-                in_=qtf(live[("abs_v", g)][:, ABS_SCALAR[g]:wide(g)]),
+                in_=qtf(live[("abs_v", g)][:, 0:wide(g) - ABS_SCALAR[g]]),
                 func=ACT.Sin, bias=halfpi[:, 0:1], scale=-1.0,
             )
 
@@ -227,17 +241,22 @@ def tile_naivefourierkanlayer_kernel(tc, x, fouriercoeffs, bias, out):
         halfpi = const.tile([P, 1], F32)
         nc.vector.tensor_scalar(out=halfpi[:], in0=quarter[:], scalar1=TWO_PI, scalar2=None, op0=ALU.mult)
 
-        xT = const.tile([P, 2, B], BF16)
+        xT = const.tile([P, 1, B], BF16)
+        xf = const.tile([P, 2, B], F32)
+        out_rows = out.rearrange("(i h) o -> i (h o)", h=2)
 
-        def transpose_x(ih):
+        def park_x(ih):
             xt_ps = xpsum.tile([P, B], BF16, name="xb")
             for bt in range(BT):
                 nc.tensor.transpose(
                     xt_ps[:, bt * P:(bt + 1) * P], xsb[:, bt, ih * P:(ih + 1) * P], ident_b[:]
                 )
-            nc.vector.tensor_copy(out=xT[:, ih, :], in_=xt_ps[:])
+            if ih == 0:
+                nc.vector.tensor_copy(out=xT[:, 0, :], in_=xt_ps[:])
+            nc.scalar.copy(out=xf[:, ih, :], in_=xt_ps[:])
+            nc.sync.dma_start(out=out_rows[ih * P:(ih + 1) * P, :], in_=xf[:, ih, :])
 
-        transpose_x(0)
+        park_x(0)
 
         y_ps = [ypsum.tile([P, O_DIM], F32, name="y%d" % bt) for bt in range(BT)]
 
@@ -248,10 +267,10 @@ def tile_naivefourierkanlayer_kernel(tc, x, fouriercoeffs, bias, out):
                 multiply(j - 1)
             if j >= -1 and ahead + 1 < N_GRP:
                 load_w(ahead + 1)
-            if ahead < N_GRP:
+                fetch_x(ahead + 1)
+            if ahead < BY_MATMUL:
                 spread_x(ahead)
-                if j < 0:
-                    copy_x(ahead)
+                copy_x(ahead)
             if j >= 0:
                 if ABS_SCALAR[j] > 0:
                     abs_scalar(j)
@@ -266,8 +285,8 @@ def tile_naivefourierkanlayer_kernel(tc, x, fouriercoeffs, bias, out):
                 cosine_v(j)
             for piece in pieces[2:]:
                 weights_piece(ahead, piece)
-            if ahead < N_GRP and j >= 0:
-                copy_x(ahead)
+            if j == -2:
+                park_x(1)
             nxt = 0 <= j + 1 < N_GRP
             if nxt:
                 angles(j + 1)
@@ -281,11 +300,9 @@ def tile_naivefourierkanlayer_kernel(tc, x, fouriercoeffs, bias, out):
                 quantise_basis(j, "cos")
             if nxt and ABS_SCALAR[j + 1] < wide(j + 1):
                 abs_vector(j + 1)
-            if j == 0:
-                transpose_x(1)
         multiply(N_GRP - 1)
 
         for bt in range(BT):
-            y_sb = two.tile([P, O_DIM], F32, name="y_sb")
+            y_sb = three.tile([P, O_DIM], F32, name="y_sb")
             nc.vector.tensor_tensor(out=y_sb[:], in0=y_ps[bt][:], in1=bias_b[:], op=ALU.add)
             nc.sync.dma_start(out=out[bt * P:(bt + 1) * P, :], in_=y_sb[:])

@@ -24,15 +24,17 @@ N_PASS = K_DIM // K_PASS
 GRP = 2
 SIZES = [1] + [GRP] * ((N_PASS - 2) // GRP) + [1]
 N_GRP = len(SIZES)
+LAST = N_GRP - 1
 FIRST = [sum(SIZES[:g]) for g in range(N_GRP)]
 COLS = GRP * B
 WIDE = COLS * PACK
 BT = B // P
 RUN = 4
-ABS_SCALAR = [B * PACK] + [2816] * (N_GRP - 3) + [1536, 512]
+ABS_SCALAR = [B * PACK] + [2624] * (N_GRP - 3) + [1536, 512]
 ABS_S_MAX = max(ABS_SCALAR)
 ABS_V_MAX = max(SIZES[g] * B * PACK - ABS_SCALAR[g] for g in range(N_GRP))
 BY_MATMUL = 2
+T_PE = PACK - 1
 
 FLOPS = 2 * B * O_DIM * 2 * K_DIM
 
@@ -57,6 +59,9 @@ def tile_naivefourierkanlayer_kernel(tc, x, fouriercoeffs, bias, out):
 
         def wide(g):
             return SIZES[g] * B * PACK
+
+        def vector_planes(g):
+            return PACK if g < BY_MATMUL else T_PE
 
         def qtf(ap):
             return ap.rearrange("p (q t f) -> p q t f", t=PACK, f=RUN)
@@ -97,6 +102,18 @@ def tile_naivefourierkanlayer_kernel(tc, x, fouriercoeffs, bias, out):
                     )
             live[("xs", g)] = xs
 
+        def angles_pe(g):
+            planes = []
+            for cc in range(SIZES[g]):
+                c = FIRST[g] + cc
+                th_ps = xpsum.tile([P, B], F32, name="xb")
+                nc.tensor.matmul(
+                    th_ps[:], lhsT=selk[:, (c % 16) * P:(c % 16 + 1) * P], rhs=xT[:, c // 16, :],
+                    start=True, stop=True,
+                )
+                planes.append(th_ps)
+            live[("theta_pe", g)] = planes
+
         def weights_piece(g, j):
             if j == 0:
                 live[("wg", g)] = two.tile([P, 2 * GRP * O_DIM * PACK], BF16, name="wg", align_bytes=64)
@@ -129,7 +146,7 @@ def tile_naivefourierkanlayer_kernel(tc, x, fouriercoeffs, bias, out):
             xs = live[("xs", g)]
             theta = one.tile([P, WIDE], F32, name="theta")
             theta_qtf = qtf(theta[:, 0:wide(g)])
-            for t in range(PACK):
+            for t in range(vector_planes(g)):
                 nc.vector.tensor_scalar(
                     out=theta_qtf[:, :, t, :], in0=xs[:, 0:SIZES[g] * B].rearrange("p (q f) -> p q f", f=RUN),
                     scalar1=kf[:, t:t + 1], scalar2=None, op0=ALU.mult,
@@ -138,18 +155,35 @@ def tile_naivefourierkanlayer_kernel(tc, x, fouriercoeffs, bias, out):
 
         def turns(g):
             nint = one.tile([P, WIDE], I32, name="nint")
+            tv = vector_planes(g)
             nc.vector.tensor_scalar(
-                out=nint[:, 0:wide(g)], in0=live[("theta", g)][:, 0:wide(g)], scalar1=INV_2PI, scalar2=None,
-                op0=ALU.mult,
+                out=qtf(nint[:, 0:wide(g)])[:, :, 0:tv, :], in0=qtf(live[("theta", g)][:, 0:wide(g)])[:, :, 0:tv, :],
+                scalar1=INV_2PI, scalar2=None, op0=ALU.mult,
             )
+            if tv < PACK:
+                nc.vector.tensor_scalar(
+                    out=qtf(nint[:, 0:wide(g)])[:, :, T_PE, :],
+                    in0=live[("xs", g)][:, 0:SIZES[g] * B].rearrange("p (q f) -> p q f", f=RUN),
+                    scalar1=turns_pe[:, 0:1], scalar2=None, op0=ALU.mult,
+                )
             live[("nint", g)] = nint
 
         def reduce_angles(g):
             arg = two.tile([P, WIDE], F32, name="arg")
+            tv = vector_planes(g)
             nc.vector.scalar_tensor_tensor(
-                out=arg[:, 0:wide(g)], in0=live[("nint", g)][:, 0:wide(g)], scalar=-TWO_PI,
-                in1=live[("theta", g)][:, 0:wide(g)], op0=ALU.mult, op1=ALU.add,
+                out=qtf(arg[:, 0:wide(g)])[:, :, 0:tv, :], in0=qtf(live[("nint", g)][:, 0:wide(g)])[:, :, 0:tv, :],
+                scalar=-TWO_PI, in1=qtf(live[("theta", g)][:, 0:wide(g)])[:, :, 0:tv, :],
+                op0=ALU.mult, op1=ALU.add,
             )
+            if tv < PACK:
+                for cc in range(SIZES[g]):
+                    cols = slice(cc * B * PACK, (cc + 1) * B * PACK)
+                    nc.vector.scalar_tensor_tensor(
+                        out=qtf(arg[:, cols])[:, :, T_PE, :], in0=qtf(live[("nint", g)][:, cols])[:, :, T_PE, :],
+                        scalar=-TWO_PI, in1=live[("theta_pe", g)][cc][:].rearrange("p (q f) -> p q f", f=RUN),
+                        op0=ALU.mult, op1=ALU.add,
+                    )
             live[("arg", g)] = arg
 
         def abs_vector(g):
@@ -196,23 +230,26 @@ def tile_naivefourierkanlayer_kernel(tc, x, fouriercoeffs, bias, out):
             )
             live[(which + "q", g)] = (codes, scales)
 
-        def multiply(g):
+        def passes(g, s, tiles, stop=False):
             wcodes, wscales = live[("w", g)]
-            for s, which in ((1, "sinq"), (0, "cosq")):
-                codes, scales = live[(which, g)]
-                for cc in range(SIZES[g]):
-                    wcol = (s * SIZES[g] + cc) * O_DIM
-                    for bt in range(BT):
-                        col = cc * B + bt * P
-                        nc.tensor.matmul_mx(
-                            out=y_ps[bt][:],
-                            lhsT=codes[:, col:col + P].bitcast(FP8X4),
-                            lhsT_scale=scales[:, col:col + P],
-                            rhs=wcodes[:, wcol:wcol + O_DIM].bitcast(FP8X4),
-                            rhs_scale=wscales[:, wcol:wcol + O_DIM],
-                            start=(g == 0 and s == 1 and cc == 0),
-                            stop=(g == N_GRP - 1 and s == 0 and cc == SIZES[g] - 1),
-                        )
+            codes, scales = live[(("cosq", "sinq")[s], g)]
+            for cc in range(SIZES[g]):
+                wcol = (s * SIZES[g] + cc) * O_DIM
+                for bt in tiles:
+                    col = cc * B + bt * P
+                    nc.tensor.matmul_mx(
+                        out=y_ps[bt][:],
+                        lhsT=codes[:, col:col + P].bitcast(FP8X4),
+                        lhsT_scale=scales[:, col:col + P],
+                        rhs=wcodes[:, wcol:wcol + O_DIM].bitcast(FP8X4),
+                        rhs_scale=wscales[:, wcol:wcol + O_DIM],
+                        start=(g == 0 and s == 1 and cc == 0),
+                        stop=(stop and cc == SIZES[g] - 1),
+                    )
+
+        def multiply(g):
+            passes(g, 1, range(BT))
+            passes(g, 0, range(BT))
 
         xsb = const.tile([P, BT, I_DIM], BF16)
         nc.sync.dma_start(out=xsb[:], in_=x.rearrange("(bt p) i -> p bt i", p=P))
@@ -232,16 +269,24 @@ def tile_naivefourierkanlayer_kernel(tc, x, fouriercoeffs, bias, out):
             out=sel[:].rearrange("p (j r) -> p j r", r=16),
             in_=ident_b[:].unsqueeze(2).to_broadcast([P, P, 16]),
         )
+        kr_i = const.tile([P, 16], I32)
+        nc.gpsimd.iota(kr_i[:], pattern=[[PACK, 16]], base=T_PE + 1, channel_multiplier=0)
+        kr = const.tile([P, 16], BF16)
+        nc.vector.tensor_copy(out=kr[:], in_=kr_i[:])
         kmod = const.tile([P, PACK], I32)
         nc.vector.tensor_single_scalar(out=kmod[:], in_=kidx[:], scalar=G_DIM - 1, op=ALU.bitwise_and)
         kf = const.tile([P, PACK], F32)
         nc.vector.tensor_scalar(out=kf[:], in0=kmod[:], scalar1=1.0, scalar2=None, op0=ALU.add)
+        turns_pe = const.tile([P, 1], F32)
+        nc.vector.tensor_scalar(
+            out=turns_pe[:], in0=kf[:, T_PE:T_PE + 1], scalar1=INV_2PI, scalar2=None, op0=ALU.mult
+        )
         quarter = const.tile([P, 1], F32)
         nc.vector.memset(quarter[:], 0.25)
         halfpi = const.tile([P, 1], F32)
         nc.vector.tensor_scalar(out=halfpi[:], in0=quarter[:], scalar1=TWO_PI, scalar2=None, op0=ALU.mult)
 
-        xT = const.tile([P, 1, B], BF16)
+        xT = const.tile([P, 2, B], BF16)
         xf = const.tile([P, 2, B], F32)
         out_rows = out.rearrange("(i h) o -> i (h o)", h=2)
 
@@ -252,15 +297,21 @@ def tile_naivefourierkanlayer_kernel(tc, x, fouriercoeffs, bias, out):
                     xt_ps[:, bt * P:(bt + 1) * P], xsb[:, bt, ih * P:(ih + 1) * P], ident_b[:]
                 )
             if ih == 0:
-                nc.vector.tensor_copy(out=xT[:, 0, :], in_=xt_ps[:])
+                nc.vector.tensor_copy(out=xT[:, ih, :], in_=xt_ps[:])
             nc.scalar.copy(out=xf[:, ih, :], in_=xt_ps[:])
             nc.sync.dma_start(out=out_rows[ih * P:(ih + 1) * P, :], in_=xf[:, ih, :])
 
         park_x(0)
+        selk = const.tile([P, P * 16], BF16)
+        nc.vector.tensor_tensor(
+            out=selk[:].rearrange("p (j r) -> p j r", r=16),
+            in0=sel[:].rearrange("p (j r) -> p j r", r=16),
+            in1=kr[:].unsqueeze(1).to_broadcast([P, P, 16]), op=ALU.mult,
+        )
 
         y_ps = [ypsum.tile([P, O_DIM], F32, name="y%d" % bt) for bt in range(BT)]
 
-        for j in range(-2, N_GRP):
+        for j in range(-2, LAST):
             ahead = j + 2
             pieces = list(range(2 * SIZES[ahead])) if ahead < N_GRP else []
             if j >= 1:
@@ -271,6 +322,8 @@ def tile_naivefourierkanlayer_kernel(tc, x, fouriercoeffs, bias, out):
             if ahead < BY_MATMUL:
                 spread_x(ahead)
                 copy_x(ahead)
+            elif ahead - 1 >= BY_MATMUL and ahead - 1 < N_GRP:
+                angles_pe(ahead - 1)
             if j >= 0:
                 if ABS_SCALAR[j] > 0:
                     abs_scalar(j)
@@ -300,9 +353,33 @@ def tile_naivefourierkanlayer_kernel(tc, x, fouriercoeffs, bias, out):
                 quantise_basis(j, "cos")
             if nxt and ABS_SCALAR[j + 1] < wide(j + 1):
                 abs_vector(j + 1)
-        multiply(N_GRP - 1)
+            if j == 0:
+                nc.vector.tensor_copy(out=xT[:, 1, :], in_=xf[:, 1, :])
 
-        for bt in range(BT):
+        multiply(LAST - 1)
+        abs_scalar(LAST)
+        cosine_s(LAST)
+        cosine_v(LAST)
+        quantise_basis(LAST, "cos")
+        passes(LAST, 0, range(BT))
+        sin_b = two.tile([P, WIDE], BF16, name="sin_b", align_bytes=64)
+        codes = two.tile([P, COLS], U32, name="sin_codes", align_bytes=64)
+        scales = two.tile([P, COLS], U8, name="sin_scales", align_bytes=64)
+        live[("sinq", LAST)] = (codes, scales)
+
+        def finish(bt):
             y_sb = three.tile([P, O_DIM], F32, name="y_sb")
             nc.vector.tensor_tensor(out=y_sb[:], in0=y_ps[bt][:], in1=bias_b[:], op=ALU.add)
             nc.sync.dma_start(out=out[bt * P:(bt + 1) * P, :], in_=y_sb[:])
+
+        for bt in range(BT):
+            cols = slice(bt * P * PACK, (bt + 1) * P * PACK)
+            nc.scalar.activation(out=qft(sin_b[:, cols]), in_=qtf(live[("arg", LAST)][:, cols]), func=ACT.Sin)
+            nc.vector.quantize_mx(
+                out=codes[:, bt * P:(bt + 1) * P].bitcast(FP8X4), scales=scales[:, bt * P:(bt + 1) * P],
+                in_=sin_b[:, cols],
+            )
+            passes(LAST, 1, [bt], stop=True)
+            if bt >= 1:
+                finish(bt - 1)
+        finish(BT - 1)

import math

import concourse.mybir as mybir
from concourse.masks import make_identity

F32 = mybir.dt.float32
BF16 = mybir.dt.bfloat16
I32 = mybir.dt.int32
U32 = mybir.dt.uint32
U8 = mybir.dt.uint8
FP8X4 = mybir.dt.float8_e4m3fn_x4
ALU = mybir.AluOpType
ACT = mybir.ActivationFunctionType

P = 128
B = 512
I_DIM = 256
O_DIM = 256
G_DIM = 64
K_DIM = I_DIM * G_DIM
PACK = 4
K_PASS = P * PACK
N_PASS = K_DIM // K_PASS
GRP = 2
SIZES = [1] + [GRP] * ((N_PASS - 2) // GRP) + [1]
N_GRP = len(SIZES)
LAST = N_GRP - 1
FIRST = [sum(SIZES[:g]) for g in range(N_GRP)]
COLS = GRP * B
WIDE = COLS * PACK
BT = B // P
RUN = 4
ABS_SCALAR = [B * PACK] + [2624] * (N_GRP - 3) + [1536, 512]
ABS_S_MAX = max(ABS_SCALAR)
ABS_V_MAX = max(SIZES[g] * B * PACK - ABS_SCALAR[g] for g in range(N_GRP))
BY_MATMUL = 2
T_PE = PACK - 1

FLOPS = 2 * B * O_DIM * 2 * K_DIM

TWO_PI = 2.0 * math.pi
INV_2PI = 1.0 / TWO_PI


def tile_naivefourierkanlayer_kernel(tc, x, fouriercoeffs, bias, out):
    nc = tc.nc
    w_view = fouriercoeffs.rearrange("s (ot o) i g -> o (s ot) (i g)", o=P)

    with tc.tile_pool(name="const", bufs=1) as const, \
            tc.tile_pool(name="two", bufs=2) as two, \
            tc.tile_pool(name="one", bufs=1) as one, \
            tc.tile_pool(name="three", bufs=3) as three, \
            tc.psum_pool(name="ypsum", bufs=1) as ypsum, \
            tc.psum_pool(name="xpsum", bufs=2) as xpsum, \
            tc.psum_pool(name="wpsum", bufs=2) as wpsum, \
            tc.manual_schedule():

        live = {}

        def wide(g):
            return SIZES[g] * B * PACK

        def vector_planes(g):
            return PACK if g < BY_MATMUL else T_PE

        def qtf(ap):
            return ap.rearrange("p (q t f) -> p q t f", t=PACK, f=RUN)

        def qft(ap):
            return ap.rearrange("p (q f t) -> p q t f", f=RUN, t=PACK)

        def load_w(g):
            wraw = two.tile([P, 4, GRP * K_PASS], BF16, name="wraw")
            nc.sync.dma_start(
                out=wraw[:, :, 0:SIZES[g] * K_PASS],
                in_=w_view[:, :, FIRST[g] * K_PASS:(FIRST[g] + SIZES[g]) * K_PASS],
            )
            live[("wraw", g)] = wraw

        def spread_x(g):
            xb_ps = xpsum.tile([P, COLS], BF16, name="xb")
            for cc in range(SIZES[g]):
                c = FIRST[g] + cc
                nc.tensor.matmul(
                    xb_ps[:, cc * B:(cc + 1) * B], lhsT=sel[:, (c % 16) * P:(c % 16 + 1) * P],
                    rhs=xT[:, c // 16, :], start=True, stop=True,
                )
            live[("xb", g)] = xb_ps

        def copy_x(g):
            xs = two.tile([P, COLS], BF16, name="xs")
            nc.scalar.copy(out=xs[:, 0:SIZES[g] * B], in_=live[("xb", g)][:, 0:SIZES[g] * B])
            live[("xs", g)] = xs

        def fetch_x(g):
            xs = three.tile([P, COLS], F32, name="xs32")
            for cc in range(SIZES[g]):
                for il in range(8):
                    nc.sync.dma_start(
                        out=xs[il * 16:(il + 1) * 16, cc * B:(cc + 1) * B],
                        in_=out_rows[(FIRST[g] + cc) * 8 + il, :].partition_broadcast(16),
                    )
            live[("xs", g)] = xs

        def angles_pe(g):
            planes = []
            for cc in range(SIZES[g]):
                c = FIRST[g] + cc
                th_ps = xpsum.tile([P, B], F32, name="xb")
                nc.tensor.matmul(
                    th_ps[:], lhsT=selk[:, (c % 16) * P:(c % 16 + 1) * P], rhs=xT[:, c // 16, :],
                    start=True, stop=True,
                )
                planes.append(th_ps)
            live[("theta_pe", g)] = planes

        def weights_piece(g, j):
            if j == 0:
                live[("wg", g)] = two.tile([P, 2 * GRP * O_DIM * PACK], BF16, name="wg", align_bytes=64)
            s, cc = divmod(j, SIZES[g])
            wwords = live[("wraw", g)][:].bitcast(F32)
            wt_ps = wpsum.tile([P, 4, P], F32, name="wt")
            for ot in range(2):
                for e in range(2):
                    nc.tensor.transpose(
                        wt_ps[:, ot * 2 + e, :],
                        wwords[:, s * 2 + ot, cc * 256 + e:(cc + 1) * 256:2],
                        ident_f[:],
                    )
            nc.scalar.copy(
                out=live[("wg", g)][:].bitcast(F32)[:, j * 512:(j + 1) * 512].rearrange(
                    "p (ot o e) -> p ot o e", ot=2, e=2),
                in_=wt_ps[:].rearrange("p (ot e) o -> p ot o e", e=2),
            )

        def quantise_w(g):
            wcodes = two.tile([P, 2 * GRP * O_DIM], U32, name="wcodes", align_bytes=64)
            wscales = two.tile([P, 2 * GRP * O_DIM], U8, name="wscales", align_bytes=64)
            n = 2 * SIZES[g] * O_DIM
            nc.vector.quantize_mx(
                out=wcodes[:, 0:n].bitcast(FP8X4), scales=wscales[:, 0:n], in_=live[("wg", g)][:, 0:n * PACK]
            )
            live[("w", g)] = (wcodes, wscales)

        def angles(g):
            xs = live[("xs", g)]
            theta = one.tile([P, WIDE], F32, name="theta")
            theta_qtf = qtf(theta[:, 0:wide(g)])
            for t in range(vector_planes(g)):
                nc.vector.tensor_scalar(
                    out=theta_qtf[:, :, t, :], in0=xs[:, 0:SIZES[g] * B].rearrange("p (q f) -> p q f", f=RUN),
                    scalar1=kf[:, t:t + 1], scalar2=None, op0=ALU.mult,
                )
            live[("theta", g)] = theta

        def turns(g):
            nint = one.tile([P, WIDE], I32, name="nint")
            tv = vector_planes(g)
            nc.vector.tensor_scalar(
                out=qtf(nint[:, 0:wide(g)])[:, :, 0:tv, :], in0=qtf(live[("theta", g)][:, 0:wide(g)])[:, :, 0:tv, :],
                scalar1=INV_2PI, scalar2=None, op0=ALU.mult,
            )
            if tv < PACK:
                nc.vector.tensor_scalar(
                    out=qtf(nint[:, 0:wide(g)])[:, :, T_PE, :],
                    in0=live[("xs", g)][:, 0:SIZES[g] * B].rearrange("p (q f) -> p q f", f=RUN),
                    scalar1=turns_pe[:, 0:1], scalar2=None, op0=ALU.mult,
                )
            live[("nint", g)] = nint

        def reduce_angles(g):
            arg = two.tile([P, WIDE], F32, name="arg")
            tv = vector_planes(g)
            nc.vector.scalar_tensor_tensor(
                out=qtf(arg[:, 0:wide(g)])[:, :, 0:tv, :], in0=qtf(live[("nint", g)][:, 0:wide(g)])[:, :, 0:tv, :],
                scalar=-TWO_PI, in1=qtf(live[("theta", g)][:, 0:wide(g)])[:, :, 0:tv, :],
                op0=ALU.mult, op1=ALU.add,
            )
            if tv < PACK:
                for cc in range(SIZES[g]):
                    cols = slice(cc * B * PACK, (cc + 1) * B * PACK)
                    nc.vector.scalar_tensor_tensor(
                        out=qtf(arg[:, cols])[:, :, T_PE, :], in0=qtf(live[("nint", g)][:, cols])[:, :, T_PE, :],
                        scalar=-TWO_PI, in1=live[("theta_pe", g)][cc][:].rearrange("p (q f) -> p q f", f=RUN),
                        op0=ALU.mult, op1=ALU.add,
                    )
            live[("arg", g)] = arg

        def abs_vector(g):
            rest = live[("arg", g)][:, ABS_SCALAR[g]:wide(g)]
            abs_v = two.tile([P, ABS_V_MAX], F32, name="abs_v")
            nc.vector.scalar_tensor_tensor(
                out=abs_v[:, 0:wide(g) - ABS_SCALAR[g]], in0=rest, scalar=-1.0, in1=rest, op0=ALU.mult, op1=ALU.max
            )
            live[("abs_v", g)] = abs_v

        def abs_scalar(g):
            abs_s = one.tile([P, ABS_S_MAX], F32, name="abs_s")
            nc.scalar.activation(
                out=abs_s[:, 0:ABS_SCALAR[g]], in_=live[("arg", g)][:, 0:ABS_SCALAR[g]], func=ACT.Abs
            )
            live[("abs_s", g)] = abs_s

        def sine(g):
            sin_b = two.tile([P, WIDE], BF16, name="sin_b", align_bytes=64)
            nc.scalar.activation(out=qft(sin_b[:, 0:wide(g)]), in_=qtf(live[("arg", g)][:, 0:wide(g)]), func=ACT.Sin)
            live[("sin", g)] = sin_b

        def cosine_s(g):
            cos_b = two.tile([P, WIDE], BF16, name="cos_b", align_bytes=64)
            nc.scalar.activation(
                out=qft(cos_b[:, 0:ABS_SCALAR[g]]), in_=qtf(live[("abs_s", g)][:, 0:ABS_SCALAR[g]]),
                func=ACT.Sin, bias=halfpi[:, 0:1], scale=-1.0,
            )
            live[("cos", g)] = cos_b

        def cosine_v(g):
            nc.scalar.activation(
                out=qft(live[("cos", g)][:, ABS_SCALAR[g]:wide(g)]),
                in_=qtf(live[("abs_v", g)][:, 0:wide(g) - ABS_SCALAR[g]]),
                func=ACT.Sin, bias=halfpi[:, 0:1], scale=-1.0,
            )

        def quantise_basis(g, which):
            codes = two.tile([P, COLS], U32, name=which + "_codes", align_bytes=64)
            scales = two.tile([P, COLS], U8, name=which + "_scales", align_bytes=64)
            n = SIZES[g] * B
            nc.vector.quantize_mx(
                out=codes[:, 0:n].bitcast(FP8X4), scales=scales[:, 0:n], in_=live[(which, g)][:, 0:n * PACK]
            )
            live[(which + "q", g)] = (codes, scales)

        def passes(g, s, tiles, stop=False):
            wcodes, wscales = live[("w", g)]
            codes, scales = live[(("cosq", "sinq")[s], g)]
            for cc in range(SIZES[g]):
                wcol = (s * SIZES[g] + cc) * O_DIM
                for bt in tiles:
                    col = cc * B + bt * P
                    nc.tensor.matmul_mx(
                        out=y_ps[bt][:],
                        lhsT=codes[:, col:col + P].bitcast(FP8X4),
                        lhsT_scale=scales[:, col:col + P],
                        rhs=wcodes[:, wcol:wcol + O_DIM].bitcast(FP8X4),
                        rhs_scale=wscales[:, wcol:wcol + O_DIM],
                        start=(g == 0 and s == 1 and cc == 0),
                        stop=(stop and cc == SIZES[g] - 1),
                    )

        def multiply(g):
            passes(g, 1, range(BT))
            passes(g, 0, range(BT))

        xsb = const.tile([P, BT, I_DIM], BF16)
        nc.sync.dma_start(out=xsb[:], in_=x.rearrange("(bt p) i -> p bt i", p=P))
        load_w(0)
        load_w(1)
        bias_b = const.tile([P, O_DIM], BF16)
        nc.sync.dma_start(out=bias_b[:], in_=bias.rearrange("o n -> (o n)").partition_broadcast(P))

        ident_b = const.tile([P, P], BF16)
        make_identity(nc, ident_b[:])
        ident_f = const.tile([P, P], F32)
        make_identity(nc, ident_f[:])
        kidx = const.tile([P, PACK], I32)
        nc.gpsimd.iota(kidx[:], pattern=[[1, PACK]], base=0, channel_multiplier=PACK)
        sel = const.tile([P, P * 16], BF16)
        nc.vector.tensor_copy(
            out=sel[:].rearrange("p (j r) -> p j r", r=16),
            in_=ident_b[:].unsqueeze(2).to_broadcast([P, P, 16]),
        )
        kr_i = const.tile([P, 16], I32)
        nc.gpsimd.iota(kr_i[:], pattern=[[PACK, 16]], base=T_PE + 1, channel_multiplier=0)
        kr = const.tile([P, 16], BF16)
        nc.vector.tensor_copy(out=kr[:], in_=kr_i[:])
        kmod = const.tile([P, PACK], I32)
        nc.vector.tensor_single_scalar(out=kmod[:], in_=kidx[:], scalar=G_DIM - 1, op=ALU.bitwise_and)
        kf = const.tile([P, PACK], F32)
        nc.vector.tensor_scalar(out=kf[:], in0=kmod[:], scalar1=1.0, scalar2=None, op0=ALU.add)
        turns_pe = const.tile([P, 1], F32)
        nc.vector.tensor_scalar(
            out=turns_pe[:], in0=kf[:, T_PE:T_PE + 1], scalar1=INV_2PI, scalar2=None, op0=ALU.mult
        )
        quarter = const.tile([P, 1], F32)
        nc.vector.memset(quarter[:], 0.25)
        halfpi = const.tile([P, 1], F32)
        nc.vector.tensor_scalar(out=halfpi[:], in0=quarter[:], scalar1=TWO_PI, scalar2=None, op0=ALU.mult)

        xT = const.tile([P, 2, B], BF16)
        xf = const.tile([P, 2, B], F32)
        out_rows = out.rearrange("(i h) o -> i (h o)", h=2)

        def park_x(ih):
            xt_ps = xpsum.tile([P, B], BF16, name="xb")
            for bt in range(BT):
                nc.tensor.transpose(
                    xt_ps[:, bt * P:(bt + 1) * P], xsb[:, bt, ih * P:(ih + 1) * P], ident_b[:]
                )
            if ih == 0:
                nc.vector.tensor_copy(out=xT[:, ih, :], in_=xt_ps[:])
            nc.scalar.copy(out=xf[:, ih, :], in_=xt_ps[:])
            nc.sync.dma_start(out=out_rows[ih * P:(ih + 1) * P, :], in_=xf[:, ih, :])

        park_x(0)
        selk = const.tile([P, P * 16], BF16)
        nc.vector.tensor_tensor(
            out=selk[:].rearrange("p (j r) -> p j r", r=16),
            in0=sel[:].rearrange("p (j r) -> p j r", r=16),
            in1=kr[:].unsqueeze(1).to_broadcast([P, P, 16]), op=ALU.mult,
        )

        y_ps = [ypsum.tile([P, O_DIM], F32, name="y%d" % bt) for bt in range(BT)]

        for j in range(-2, LAST):
            ahead = j + 2
            pieces = list(range(2 * SIZES[ahead])) if ahead < N_GRP else []
            if j >= 1:
                multiply(j - 1)
            if j >= -1 and ahead + 1 < N_GRP:
                load_w(ahead + 1)
                fetch_x(ahead + 1)
            if ahead < BY_MATMUL:
                spread_x(ahead)
                copy_x(ahead)
            elif ahead - 1 >= BY_MATMUL and ahead - 1 < N_GRP:
                angles_pe(ahead - 1)
            if j >= 0:
                if ABS_SCALAR[j] > 0:
                    abs_scalar(j)
                sine(j)
            for piece in pieces[0:1]:
                weights_piece(ahead, piece)
            if j >= 0:
                cosine_s(j)
            for piece in pieces[1:2]:
                weights_piece(ahead, piece)
            if j >= 0 and ABS_SCALAR[j] < wide(j):
                cosine_v(j)
            for piece in pieces[2:]:
                weights_piece(ahead, piece)
            if j == -2:
                park_x(1)
            nxt = 0 <= j + 1 < N_GRP
            if nxt:
                angles(j + 1)
                quantise_w(j + 1)
                turns(j + 1)
            if j >= 0:
                quantise_basis(j, "sin")
            if nxt:
                reduce_angles(j + 1)
            if j >= 0:
                quantise_basis(j, "cos")
            if nxt and ABS_SCALAR[j + 1] < wide(j + 1):
                abs_vector(j + 1)
            if j == 0:
                nc.vector.tensor_copy(out=xT[:, 1, :], in_=xf[:, 1, :])

        multiply(LAST - 1)
        abs_scalar(LAST)
        cosine_s(LAST)
        cosine_v(LAST)
        quantise_basis(LAST, "cos")
        passes(LAST, 0, range(BT))
        sin_b = two.tile([P, WIDE], BF16, name="sin_b", align_bytes=64)
        codes = two.tile([P, COLS], U32, name="sin_codes", align_bytes=64)
        scales = two.tile([P, COLS], U8, name="sin_scales", align_bytes=64)
        live[("sinq", LAST)] = (codes, scales)

        def finish(bt):
            y_sb = three.tile([P, O_DIM], F32, name="y_sb")
            nc.vector.tensor_tensor(out=y_sb[:], in0=y_ps[bt][:], in1=bias_b[:], op=ALU.add)
            nc.sync.dma_start(out=out[bt * P:(bt + 1) * P, :], in_=y_sb[:])

        for bt in range(BT):
            cols = slice(bt * P * PACK, (bt + 1) * P * PACK)
            nc.scalar.activation(out=qft(sin_b[:, cols]), in_=qtf(live[("arg", LAST)][:, cols]), func=ACT.Sin)
            nc.vector.quantize_mx(
                out=codes[:, bt * P:(bt + 1) * P].bitcast(FP8X4), scales=scales[:, bt * P:(bt + 1) * P],
                in_=sin_b[:, cols],
            )
            passes(LAST, 1, [bt], stop=True)
            if bt >= 1:
                finish(bt - 1)
        finish(BT - 1)
